import numpy as np
import ml_dtypes


def mxq(x, axis, fmt="e4m3"):
    dtype, down = {"e4m3": (ml_dtypes.float8_e4m3fn, 7), "e5m2": (ml_dtypes.float8_e5m2, 14)}[fmt]
    v = np.moveaxis(np.asarray(x, np.float32).astype(ml_dtypes.bfloat16).astype(np.float64), axis, -1)
    blocks = v.reshape(v.shape[:-1] + (-1, 32))
    amax = np.abs(blocks).max(-1, keepdims=True)
    byte = np.maximum(np.where(amax > 0, np.frexp(amax)[1] - 1 + 127, 0) - down, 1)
    scale = np.exp2(byte - 127.0)
    codes = (blocks / scale).astype(np.float32).astype(dtype).astype(np.float64)
    return np.moveaxis((codes * scale).reshape(v.shape), -1, axis)


WIDE = False


def mx_kscale(k):
    if not WIDE:
        return np.ones(k)
    levels = np.array([10, -10, 5, -5, 0])
    a = np.random.permutation(np.resize(levels, k // 512 * 4)).reshape(k // 512, 4)
    idx = np.arange(k)
    return np.exp2(a[idx // 512, idx % 128 // 32])


BF16 = ml_dtypes.bfloat16


def bf(x):
    return np.asarray(x, np.float32).astype(BF16)


def f64(x):
    return np.asarray(x).astype(np.float64)


N, D, T, H, DH = 1, 1024, 512, 2, 512
EPS = 1e-12
A = 6.0
R = 0.2


def l2norm(x):
    n = np.sqrt(np.sum(x * x, axis=-1, keepdims=True))
    return x / np.maximum(n, EPS)


def setup_inputs():
    s = mx_kscale(D)
    return {"rgb": bf(np.random.standard_normal((N, D, T)) * R * s[None, :, None]),
            "rgb_proj": bf(np.random.standard_normal((H, D, DH)) / (R * np.sqrt(D)) / s[None, :, None]),
            "atte_w": bf(np.random.standard_normal((H, DH, DH)) * A)}


def reference(rgb, rgb_proj, atte_w):
    rgb_t = f64(rgb).swapaxes(1, 2)
    p = mxq(rgb_t, 2, "e4m3")[:, None] @ mxq(f64(rgb_proj), 1, "e4m3")[None]
    o_rgb = l2norm(p)
    q_bil = mxq(o_rgb, 3, "e4m3") @ mxq(f64(atte_w), 1, "e4m3")[None]
    return o_rgb, q_bil

@@ -1,0 +1,260 @@
+from contextlib import ExitStack
+
+import concourse.masks as masks
+import concourse.mybir as mybir
+
+F32 = mybir.dt.float32
+BF16 = mybir.dt.bfloat16
+U32 = mybir.dt.uint32
+U8 = mybir.dt.uint8
+FP8X4 = mybir.dt.float8_e4m3fn_x4
+ACT = mybir.ActivationFunctionType
+
+P = 128
+PACK = 4
+K_PASS = P * PACK
+D, T, H, DH = 1024, 512, 2, 512
+TT = T // P
+UNITS = H * TT
+FLOOR = 1e-24
+FLOPS = 2 * H * T * D * DH + 2 * H * T * DH * DH
+
+
+def tile_mca_pa_kernel(tc, rgb, rgb_proj, atte_w, out_0, out_1):
+    nc = tc.nc
+    with ExitStack() as ctx:
+        keep = ctx.enter_context(tc.tile_pool(name="keep", bufs=1))
+        junkp = ctx.enter_context(tc.tile_pool(name="junkp", bufs=2))
+        psum = ctx.enter_context(tc.psum_pool(name="psum", bufs=1))
+        ctx.enter_context(tc.manual_schedule())
+
+        rgb_rows = rgb.rearrange("n d t -> (n d) t")
+        proj_rows = rgb_proj.rearrange("h d f -> (h d) f")
+        w_view = atte_w.rearrange("h (j p) n -> h p j n", p=P)
+        o_view = out_0.rearrange("n h (i p) f -> (n h i) p f", p=P)
+        q_view = out_1.rearrange("n h (i p) f -> (n h i) p f", p=P)
+
+        def k_first(rows, c):
+            return rows[c * K_PASS : (c + 1) * K_PASS, :].rearrange("(p j) w -> p j w", j=PACK)
+
+        sources = {
+            "b0": k_first(proj_rows, 0),
+            "a0": k_first(rgb_rows, 0),
+            "b1": k_first(proj_rows, 1),
+            "a1": k_first(rgb_rows, 1),
+            "c0": k_first(proj_rows, 2),
+            "c1": k_first(proj_rows, 3),
+            "w0": w_view[0],
+            "w1": w_view[1],
+        }
+        order = ["b0", "a0", "b1", "a1", "c0", "c1", "w0", "w1"]
+
+        warm = keep.tile([P, 1], F32, name="warm")
+        nc.vector.memset(warm[:], 1.0)
+        nc.scalar.activation(out=warm[:], in_=warm[:], func=ACT.Abs_reciprocal_sqrt)
+
+        raw, grouped, codes, scales = {}, {}, {}, {}
+        for k in order:
+            raw[k] = keep.tile([P, PACK, 512], BF16, name="raw_" + k)
+            grouped[k] = keep.tile([P, 512, PACK], BF16, name="grp_" + k, align_bytes=64)
+            codes[k] = keep.tile([P, 512], U32, name="cod_" + k, align_bytes=64)
+            scales[k] = keep.tile([P, 512], U8, name="scl_" + k, align_bytes=64)
+            nc.sync.dma_start(out=raw[k][:], in_=sources[k])
+
+        ident = keep.tile([P, P], F32, name="ident")
+        masks.make_identity(nc, ident[:])
+
+        def regroup(engine_copy, k, lo, hi):
+            engine_copy(
+                out=grouped[k][:, lo:hi, :].rearrange("p (c i) j -> p c j i", i=4),
+                in_=raw[k][:, :, lo:hi].rearrange("p j (c i) -> p c j i", i=4),
+            )
+
+        def rg_v(k, lo, hi):
+            regroup(nc.vector.tensor_copy, k, lo, hi)
+
+        def rg_s(k, lo, hi):
+            regroup(nc.scalar.copy, k, lo, hi)
+
+        def quantise(k, lo, hi):
+            nc.vector.quantize_mx(
+                out=codes[k][:, lo:hi].bitcast(FP8X4),
+                scales=scales[k][:, lo:hi],
+                in_=grouped[k][:, lo:hi, :].rearrange("p w j -> p (w j)"),
+            )
+
+        ssq = keep.tile([P, UNITS], F32, name="ssq")
+        clamped = keep.tile([P, UNITS], F32, name="clamped")
+        rnorm = keep.tile([P, UNITS], F32, name="rnorm")
+        p_ps, x_ps, q_ps, o_sb, q_sb, og, oc, osc = {}, {}, {}, {}, {}, {}, {}, {}
+
+        def project(u, c):
+            h, i = divmod(u, TT)
+            a, b = ("a%d" % c), (("b%d" if h == 0 else "c%d") % c)
+            if c == 0:
+                p_ps[u] = psum.tile([P, DH], F32, name="p%d" % u, tag="bank%d" % u)
+            nc.tensor.matmul_mx(
+                out=p_ps[u][:],
+                lhsT=codes[a][:, i * P : (i + 1) * P].bitcast(FP8X4),
+                lhsT_scale=scales[a][:, i * P : (i + 1) * P],
+                rhs=codes[b][:].bitcast(FP8X4),
+                rhs_scale=scales[b][:],
+                start=(c == 0),
+                stop=(c == 1),
+            )
+
+        def sum_squares(u):
+            junk = junkp.tile([P, DH], BF16, name="junk")
+            nc.scalar.activation(
+                out=junk[:], in_=p_ps[u][:], func=ACT.Square, accum_out=ssq[:, u : u + 1]
+            )
+
+        def clamp(lo, hi):
+            nc.scalar.activation(
+                out=clamped[:, lo:hi], in_=ssq[:, lo:hi], func=ACT.Relu, bias=-FLOOR
+            )
+
+        def inverse_norm(lo, hi):
+            nc.scalar.activation(
+                out=rnorm[:, lo:hi], in_=clamped[:, lo:hi], func=ACT.Abs_reciprocal_sqrt, bias=FLOOR
+            )
+
+        def scale_store_transpose(u):
+            o_sb[u] = keep.tile([P, DH], F32, name="o_sb%d" % u)
+            nc.scalar.activation(
+                out=o_sb[u][:], in_=p_ps[u][:], func=ACT.Copy, scale=rnorm[:, u : u + 1]
+            )
+            nc.sync.dma_start(out=o_view[u], in_=o_sb[u][:])
+            x_ps[u] = psum.tile([P, PACK, P], F32, name="x%d" % u, tag="bank%d" % u)
+            for j in range(PACK):
+                nc.tensor.transpose(x_ps[u][:, j, :], o_sb[u][:, j * P : (j + 1) * P], ident[:])
+
+        def evacuate_transposed(engine_copy, u):
+            og[u] = keep.tile([P, P, PACK], BF16, name="og%d" % u, align_bytes=64)
+            engine_copy(out=og[u][:], in_=x_ps[u][:].rearrange("p j t -> p t j"))
+
+        def quantise_o(u):
+            oc[u] = keep.tile([P, P], U32, name="oc%d" % u, align_bytes=64)
+            osc[u] = keep.tile([P, P], U8, name="osc%d" % u, align_bytes=64)
+            nc.vector.quantize_mx(
+                out=oc[u][:].bitcast(FP8X4),
+                scales=osc[u][:],
+                in_=og[u][:].rearrange("p t j -> p (t j)"),
+            )
+
+        def bilinear(u):
+            w = "w%d" % (u // TT)
+            q_ps[u] = psum.tile([P, DH], F32, name="q%d" % u, tag="bank%d" % u)
+            nc.tensor.matmul_mx(
+                out=q_ps[u][:],
+                lhsT=oc[u][:].bitcast(FP8X4),
+                lhsT_scale=osc[u][:],
+                rhs=codes[w][:].bitcast(FP8X4),
+                rhs_scale=scales[w][:],
+                start=True,
+                stop=True,
+            )
+
+        def store_q(engine_copy, u):
+            q_sb[u] = keep.tile([P, DH], F32, name="q_sb%d" % u)
+            engine_copy(out=q_sb[u][:], in_=q_ps[u][:])
+            nc.sync.dma_start(out=q_view[u], in_=q_sb[u][:])
+
+        def prepare(k):
+            rg_v(k, 0, 256)
+            rg_v(k, 256, 512)
+            quantise(k, 0, 512)
+
+        vcopy, scopy = nc.vector.tensor_copy, nc.scalar.copy
+
+        rg_v("b0", 0, 256)
+        rg_s("b0", 256, 512)
+        quantise("b0", 0, 256)
+        rg_v("a0", 0, 256)
+        rg_s("a0", 256, 512)
+        quantise("b0", 256, 512)
+        quantise("a0", 0, 256)
+        rg_v("b1", 0, 256)
+        rg_s("b1", 256, 512)
+        quantise("a0", 256, 512)
+        for u in range(TT):
+            project(u, 0)
+        quantise("b1", 0, 256)
+        rg_v("a1", 0, 128)
+        rg_s("a1", 128, 256)
+        quantise("b1", 256, 512)
+        quantise("a1", 0, 128)
+        project(0, 1)
+        rg_v("a1", 256, 384)
+        rg_s("a1", 384, 512)
+        for i in range(1, TT):
+            quantise("a1", i * P, (i + 1) * P)
+            project(i, 1)
+
+        prepare("c0")
+        for u in range(TT, UNITS):
+            project(u, 0)
+        sum_squares(0)
+        sum_squares(1)
+        sum_squares(2)
+        clamp(0, 2)
+        sum_squares(3)
+        inverse_norm(0, 2)
+        clamp(2, 4)
+        scale_store_transpose(0)
+        prepare("c1")
+        for u in range(TT, UNITS):
+            project(u, 1)
+        inverse_norm(2, 4)
+        scale_store_transpose(1)
+        scale_store_transpose(2)
+        scale_store_transpose(3)
+        prepare("w0")
+
+        evacuate_transposed(vcopy, 0)
+        evacuate_transposed(vcopy, 1)
+        quantise_o(0)
+        bilinear(0)
+        evacuate_transposed(vcopy, 2)
+        quantise_o(1)
+        bilinear(1)
+        evacuate_transposed(vcopy, 3)
+        quantise_o(2)
+        bilinear(2)
+        sum_squares(4)
+        sum_squares(5)
+        sum_squares(6)
+        clamp(4, 6)
+        sum_squares(7)
+        inverse_norm(4, 6)
+        clamp(6, 8)
+        store_q(vcopy, 0)
+        quantise_o(3)
+        bilinear(3)
+        scale_store_transpose(4)
+        inverse_norm(6, 8)
+        store_q(vcopy, 1)
+        scale_store_transpose(5)
+        store_q(vcopy, 2)
+        scale_store_transpose(6)
+        rg_v("w1", 0, 256)
+        evacuate_transposed(scopy, 4)
+        store_q(vcopy, 3)
+        scale_store_transpose(7)
+        rg_v("w1", 256, 512)
+        quantise_o(4)
+        quantise("w1", 0, 512)
+        bilinear(4)
+        evacuate_transposed(scopy, 5)
+        quantise_o(5)
+        bilinear(5)
+        evacuate_transposed(scopy, 6)
+        quantise_o(6)
+        bilinear(6)
+        store_q(vcopy, 4)
+        evacuate_transposed(scopy, 7)
+        quantise_o(7)
+        bilinear(7)
+        store_q(scopy, 5)
+        store_q(vcopy, 6)
+        store_q(vcopy, 7)

@@ -160,11 +160,6 @@ def tile_mca_pa_kernel(tc, rgb, rgb_proj, atte_w, out_0, out_1):
             engine_copy(out=q_sb[u][:], in_=q_ps[u][:])
             nc.sync.dma_start(out=q_view[u], in_=q_sb[u][:])
 
-        def prepare(k):
-            rg_v(k, 0, 256)
-            rg_v(k, 256, 512)
-            quantise(k, 0, 512)
-
         vcopy, scopy = nc.vector.tensor_copy, nc.scalar.copy
 
         rg_v("b0", 0, 256)
@@ -191,7 +186,10 @@ def tile_mca_pa_kernel(tc, rgb, rgb_proj, atte_w, out_0, out_1):
             quantise("a1", i * P, (i + 1) * P)
             project(i, 1)
 
-        prepare("c0")
+        rg_v("c0", 0, 256)
+        rg_v("c0", 256, 512)
+        rg_v("c1", 0, 256)
+        quantise("c0", 0, 512)
         for u in range(TT, UNITS):
             project(u, 0)
         sum_squares(0)
@@ -202,16 +200,19 @@ def tile_mca_pa_kernel(tc, rgb, rgb_proj, atte_w, out_0, out_1):
         inverse_norm(0, 2)
         clamp(2, 4)
         scale_store_transpose(0)
-        prepare("c1")
+        rg_v("c1", 256, 512)
+        rg_v("w0", 0, 256)
+        quantise("c1", 0, 512)
         for u in range(TT, UNITS):
             project(u, 1)
         inverse_norm(2, 4)
         scale_store_transpose(1)
         scale_store_transpose(2)
         scale_store_transpose(3)
-        prepare("w0")
+        rg_v("w0", 256, 512)
 
         evacuate_transposed(vcopy, 0)
+        quantise("w0", 0, 512)
         evacuate_transposed(vcopy, 1)
         quantise_o(0)
         bilinear(0)

@@ -200,13 +200,13 @@ def tile_mca_pa_kernel(tc, rgb, rgb_proj, atte_w, out_0, out_1):
         inverse_norm(0, 2)
         clamp(2, 4)
         scale_store_transpose(0)
+        inverse_norm(2, 4)
+        scale_store_transpose(1)
         rg_v("c1", 256, 512)
         rg_v("w0", 0, 256)
         quantise("c1", 0, 512)
         for u in range(TT, UNITS):
             project(u, 1)
-        inverse_norm(2, 4)
-        scale_store_transpose(1)
         scale_store_transpose(2)
         scale_store_transpose(3)
         rg_v("w0", 256, 512)
@@ -229,33 +229,33 @@ def tile_mca_pa_kernel(tc, rgb, rgb_proj, atte_w, out_0, out_1):
         sum_squares(7)
         inverse_norm(4, 6)
         clamp(6, 8)
+        scale_store_transpose(4)
         store_q(vcopy, 0)
         quantise_o(3)
         bilinear(3)
-        scale_store_transpose(4)
         inverse_norm(6, 8)
-        store_q(vcopy, 1)
         scale_store_transpose(5)
-        store_q(vcopy, 2)
+        store_q(vcopy, 1)
         scale_store_transpose(6)
-        rg_v("w1", 0, 256)
-        evacuate_transposed(scopy, 4)
-        store_q(vcopy, 3)
         scale_store_transpose(7)
+        rg_v("w1", 0, 256)
         rg_v("w1", 256, 512)
-        quantise_o(4)
+        store_q(vcopy, 2)
         quantise("w1", 0, 512)
+        evacuate_transposed(scopy, 4)
+        quantise_o(4)
         bilinear(4)
+        store_q(vcopy, 3)
         evacuate_transposed(scopy, 5)
         quantise_o(5)
         bilinear(5)
         evacuate_transposed(scopy, 6)
         quantise_o(6)
         bilinear(6)
-        store_q(vcopy, 4)
         evacuate_transposed(scopy, 7)
         quantise_o(7)
         bilinear(7)
+        store_q(vcopy, 4)
         store_q(scopy, 5)
-        store_q(vcopy, 6)
+        store_q(scopy, 6)
         store_q(vcopy, 7)

@@ -119,12 +119,19 @@ def tile_mca_pa_kernel(tc, rgb, rgb_proj, atte_w, out_0, out_1):
                 out=rnorm[:, lo:hi], in_=clamped[:, lo:hi], func=ACT.Abs_reciprocal_sqrt, bias=FLOOR
             )
 
-        def scale_store_transpose(u):
+        def scale(engine, u):
             o_sb[u] = keep.tile([P, DH], F32, name="o_sb%d" % u)
-            nc.scalar.activation(
-                out=o_sb[u][:], in_=p_ps[u][:], func=ACT.Copy, scale=rnorm[:, u : u + 1]
-            )
+            if engine == "S":
+                nc.scalar.activation(
+                    out=o_sb[u][:], in_=p_ps[u][:], func=ACT.Copy, scale=rnorm[:, u : u + 1]
+                )
+            else:
+                nc.vector.tensor_scalar_mul(out=o_sb[u][:], in0=p_ps[u][:], scalar1=rnorm[:, u : u + 1])
+
+        def store_o(u):
             nc.sync.dma_start(out=o_view[u], in_=o_sb[u][:])
+
+        def transposes(u):
             x_ps[u] = psum.tile([P, PACK, P], F32, name="x%d" % u, tag="bank%d" % u)
             for j in range(PACK):
                 nc.tensor.transpose(x_ps[u][:, j, :], o_sb[u][:, j * P : (j + 1) * P], ident[:])
@@ -155,9 +162,11 @@ def tile_mca_pa_kernel(tc, rgb, rgb_proj, atte_w, out_0, out_1):
                 stop=True,
             )
 
-        def store_q(engine_copy, u):
+        def copy_q(engine_copy, u):
             q_sb[u] = keep.tile([P, DH], F32, name="q_sb%d" % u)
             engine_copy(out=q_sb[u][:], in_=q_ps[u][:])
+
+        def store_q(u):
             nc.sync.dma_start(out=q_view[u], in_=q_sb[u][:])
 
         vcopy, scopy = nc.vector.tensor_copy, nc.scalar.copy
@@ -169,93 +178,125 @@ def tile_mca_pa_kernel(tc, rgb, rgb_proj, atte_w, out_0, out_1):
         rg_s("a0", 256, 512)
         quantise("b0", 256, 512)
         quantise("a0", 0, 256)
-        rg_v("b1", 0, 256)
         rg_s("b1", 256, 512)
+        rg_v("b1", 0, 256)
+        project(0, 0)
         quantise("a0", 256, 512)
-        for u in range(TT):
-            project(u, 0)
+        project(1, 0)
         quantise("b1", 0, 256)
-        rg_v("a1", 0, 128)
         rg_s("a1", 128, 256)
+        rg_v("a1", 0, 128)
+        project(2, 0)
         quantise("b1", 256, 512)
-        quantise("a1", 0, 128)
-        project(0, 1)
-        rg_v("a1", 256, 384)
+        project(3, 0)
         rg_s("a1", 384, 512)
-        for i in range(1, TT):
-            quantise("a1", i * P, (i + 1) * P)
-            project(i, 1)
-
-        rg_v("c0", 0, 256)
-        rg_v("c0", 256, 512)
-        rg_v("c1", 0, 256)
-        quantise("c0", 0, 512)
-        for u in range(TT, UNITS):
-            project(u, 0)
+        quantise("a1", 0, 128)
+        rg_v("a1", 256, 384)
+        rg_s("c0", 384, 512)
+        quantise("a1", 128, 256)
+        project(0, 1)
+        quantise("a1", 256, 384)
+        quantise("a1", 384, 512)
+        rg_v("c0", 0, 192)
+        project(1, 1)
         sum_squares(0)
+        project(2, 1)
+        rg_v("c0", 192, 384)
+        project(3, 1)
         sum_squares(1)
+        rg_v("c1", 0, 256)
         sum_squares(2)
+        quantise("c0", 0, 512)
         clamp(0, 2)
         sum_squares(3)
-        inverse_norm(0, 2)
-        clamp(2, 4)
-        scale_store_transpose(0)
-        inverse_norm(2, 4)
-        scale_store_transpose(1)
         rg_v("c1", 256, 512)
+        project(4, 0)
+        inverse_norm(0, 2)
         rg_v("w0", 0, 256)
+        clamp(2, 4)
+        project(5, 0)
+        scale("S", 0)
+        store_o(0)
+        project(6, 0)
+        project(7, 0)
         quantise("c1", 0, 512)
-        for u in range(TT, UNITS):
-            project(u, 1)
-        scale_store_transpose(2)
-        scale_store_transpose(3)
+        inverse_norm(2, 4)
+        scale("S", 1)
+        store_o(1)
+        transposes(0)
         rg_v("w0", 256, 512)
-
+        scale("S", 2)
+        store_o(2)
+        transposes(1)
         evacuate_transposed(vcopy, 0)
+        scale("S", 3)
+        store_o(3)
+        project(4, 1)
         quantise("w0", 0, 512)
-        evacuate_transposed(vcopy, 1)
-        quantise_o(0)
-        bilinear(0)
-        evacuate_transposed(vcopy, 2)
-        quantise_o(1)
-        bilinear(1)
-        evacuate_transposed(vcopy, 3)
-        quantise_o(2)
-        bilinear(2)
+        project(5, 1)
+        project(6, 1)
         sum_squares(4)
+        evacuate_transposed(vcopy, 1)
+        project(7, 1)
+        transposes(2)
         sum_squares(5)
+        quantise_o(0)
+        transposes(3)
         sum_squares(6)
+        evacuate_transposed(vcopy, 2)
+        bilinear(0)
+        quantise_o(1)
         clamp(4, 6)
         sum_squares(7)
+        evacuate_transposed(vcopy, 3)
+        bilinear(1)
         inverse_norm(4, 6)
+        quantise_o(2)
         clamp(6, 8)
-        scale_store_transpose(4)
-        store_q(vcopy, 0)
+        scale("S", 4)
+        store_o(4)
+        copy_q(vcopy, 0)
+        store_q(0)
+        bilinear(2)
         quantise_o(3)
-        bilinear(3)
         inverse_norm(6, 8)
-        scale_store_transpose(5)
-        store_q(vcopy, 1)
-        scale_store_transpose(6)
-        scale_store_transpose(7)
+        scale("S", 5)
+        store_o(5)
+        transposes(4)
+        copy_q(vcopy, 1)
+        store_q(1)
+        bilinear(3)
         rg_v("w1", 0, 256)
+        scale("S", 6)
+        store_o(6)
+        transposes(5)
         rg_v("w1", 256, 512)
-        store_q(vcopy, 2)
-        quantise("w1", 0, 512)
+        scale("S", 7)
+        store_o(7)
+        transposes(6)
+        copy_q(vcopy, 2)
+        store_q(2)
         evacuate_transposed(scopy, 4)
-        quantise_o(4)
-        bilinear(4)
-        store_q(vcopy, 3)
+        transposes(7)
+        quantise("w1", 0, 512)
         evacuate_transposed(scopy, 5)
-        quantise_o(5)
-        bilinear(5)
+        quantise_o(4)
+        copy_q(vcopy, 3)
+        store_q(3)
         evacuate_transposed(scopy, 6)
-        quantise_o(6)
-        bilinear(6)
+        bilinear(4)
+        quantise_o(5)
         evacuate_transposed(scopy, 7)
+        quantise_o(6)
+        copy_q(vcopy, 4)
+        store_q(4)
+        bilinear(5)
+        bilinear(6)
         quantise_o(7)
+        copy_q(scopy, 5)
+        store_q(5)
+        copy_q(vcopy, 6)
+        store_q(6)
         bilinear(7)
-        store_q(vcopy, 4)
-        store_q(scopy, 5)
-        store_q(scopy, 6)
-        store_q(vcopy, 7)
+        copy_q(vcopy, 7)
+        store_q(7)

@@ -169,6 +169,27 @@ def tile_mca_pa_kernel(tc, rgb, rgb_proj, atte_w, out_0, out_1):
         def store_q(u):
             nc.sync.dma_start(out=q_view[u], in_=q_sb[u][:])
 
+        HALF = DH // 2
+        qh_ps, qh_sb = {}, {}
+
+        def bilinear_half(u, s, bank):
+            w = "w%d" % (u // TT)
+            qh_ps[s] = psum.tile([P, HALF], F32, name="qh%d" % s, tag="bank%d" % bank)
+            nc.tensor.matmul_mx(
+                out=qh_ps[s][:],
+                lhsT=oc[u][:].bitcast(FP8X4),
+                lhsT_scale=osc[u][:],
+                rhs=codes[w][:, s * HALF : (s + 1) * HALF].bitcast(FP8X4),
+                rhs_scale=scales[w][:, s * HALF : (s + 1) * HALF],
+                start=True,
+                stop=True,
+            )
+
+        def copy_store_half(engine_copy, u, s):
+            qh_sb[s] = keep.tile([P, HALF], F32, name="qh_sb%d" % s)
+            engine_copy(out=qh_sb[s][:], in_=qh_ps[s][:])
+            nc.sync.dma_start(out=q_view[u][:, s * HALF : (s + 1) * HALF], in_=qh_sb[s][:])
+
         vcopy, scopy = nc.vector.tensor_copy, nc.scalar.copy
 
         rg_v("b0", 0, 256)
@@ -297,6 +318,7 @@ def tile_mca_pa_kernel(tc, rgb, rgb_proj, atte_w, out_0, out_1):
         store_q(5)
         copy_q(vcopy, 6)
         store_q(6)
-        bilinear(7)
-        copy_q(vcopy, 7)
-        store_q(7)
+        bilinear_half(7, 0, 7)
+        bilinear_half(7, 1, 3)
+        copy_store_half(vcopy, 7, 0)
+        copy_store_half(scopy, 7, 1)

@@ -26,7 +26,6 @@ def tile_mca_pa_kernel(tc, rgb, rgb_proj, atte_w, out_0, out_1):
         keep = ctx.enter_context(tc.tile_pool(name="keep", bufs=1))
         junkp = ctx.enter_context(tc.tile_pool(name="junkp", bufs=2))
         psum = ctx.enter_context(tc.psum_pool(name="psum", bufs=1))
-        ctx.enter_context(tc.manual_schedule())
 
         rgb_rows = rgb.rearrange("n d t -> (n d) t")
         proj_rows = rgb_proj.rearrange("h d f -> (h d) f")
@@ -119,19 +118,12 @@ def tile_mca_pa_kernel(tc, rgb, rgb_proj, atte_w, out_0, out_1):
                 out=rnorm[:, lo:hi], in_=clamped[:, lo:hi], func=ACT.Abs_reciprocal_sqrt, bias=FLOOR
             )
 
-        def scale(engine, u):
+        def scale_store_transpose(u):
             o_sb[u] = keep.tile([P, DH], F32, name="o_sb%d" % u)
-            if engine == "S":
-                nc.scalar.activation(
-                    out=o_sb[u][:], in_=p_ps[u][:], func=ACT.Copy, scale=rnorm[:, u : u + 1]
-                )
-            else:
-                nc.vector.tensor_scalar_mul(out=o_sb[u][:], in0=p_ps[u][:], scalar1=rnorm[:, u : u + 1])
-
-        def store_o(u):
+            nc.scalar.activation(
+                out=o_sb[u][:], in_=p_ps[u][:], func=ACT.Copy, scale=rnorm[:, u : u + 1]
+            )
             nc.sync.dma_start(out=o_view[u], in_=o_sb[u][:])
-
-        def transposes(u):
             x_ps[u] = psum.tile([P, PACK, P], F32, name="x%d" % u, tag="bank%d" % u)
             for j in range(PACK):
                 nc.tensor.transpose(x_ps[u][:, j, :], o_sb[u][:, j * P : (j + 1) * P], ident[:])
@@ -162,33 +154,10 @@ def tile_mca_pa_kernel(tc, rgb, rgb_proj, atte_w, out_0, out_1):
                 stop=True,
             )
 
-        def copy_q(engine_copy, u):
+        def store_q(engine_copy, u):
             q_sb[u] = keep.tile([P, DH], F32, name="q_sb%d" % u)
             engine_copy(out=q_sb[u][:], in_=q_ps[u][:])
-
-        def store_q(u):
             nc.sync.dma_start(out=q_view[u], in_=q_sb[u][:])
-
-        HALF = DH // 2
-        qh_ps, qh_sb = {}, {}
-
-        def bilinear_half(u, s, bank):
-            w = "w%d" % (u // TT)
-            qh_ps[s] = psum.tile([P, HALF], F32, name="qh%d" % s, tag="bank%d" % bank)
-            nc.tensor.matmul_mx(
-                out=qh_ps[s][:],
-                lhsT=oc[u][:].bitcast(FP8X4),
-                lhsT_scale=osc[u][:],
-                rhs=codes[w][:, s * HALF : (s + 1) * HALF].bitcast(FP8X4),
-                rhs_scale=scales[w][:, s * HALF : (s + 1) * HALF],
-                start=True,
-                stop=True,
-            )
-
-        def copy_store_half(engine_copy, u, s):
-            qh_sb[s] = keep.tile([P, HALF], F32, name="qh_sb%d" % s)
-            engine_copy(out=qh_sb[s][:], in_=qh_ps[s][:])
-            nc.sync.dma_start(out=q_view[u][:, s * HALF : (s + 1) * HALF], in_=qh_sb[s][:])
 
         vcopy, scopy = nc.vector.tensor_copy, nc.scalar.copy
 
@@ -199,126 +168,93 @@ def tile_mca_pa_kernel(tc, rgb, rgb_proj, atte_w, out_0, out_1):
         rg_s("a0", 256, 512)
         quantise("b0", 256, 512)
         quantise("a0", 0, 256)
-        rg_s("b1", 256, 512)
         rg_v("b1", 0, 256)
-        project(0, 0)
+        rg_s("b1", 256, 512)
         quantise("a0", 256, 512)
-        project(1, 0)
+        for u in range(TT):
+            project(u, 0)
         quantise("b1", 0, 256)
-        rg_s("a1", 128, 256)
         rg_v("a1", 0, 128)
-        project(2, 0)
+        rg_s("a1", 128, 256)
         quantise("b1", 256, 512)
-        project(3, 0)
-        rg_s("a1", 384, 512)
         quantise("a1", 0, 128)
-        rg_v("a1", 256, 384)
-        rg_s("c0", 384, 512)
-        quantise("a1", 128, 256)
         project(0, 1)
-        quantise("a1", 256, 384)
-        quantise("a1", 384, 512)
-        rg_v("c0", 0, 192)
-        project(1, 1)
-        sum_squares(0)
-        project(2, 1)
-        rg_v("c0", 192, 384)
-        project(3, 1)
-        sum_squares(1)
+        rg_v("a1", 256, 384)
+        rg_s("a1", 384, 512)
+        for i in range(1, TT):
+            quantise("a1", i * P, (i + 1) * P)
+            project(i, 1)
+
+        rg_v("c0", 0, 256)
+        rg_v("c0", 256, 512)
         rg_v("c1", 0, 256)
-        sum_squares(2)
         quantise("c0", 0, 512)
+        for u in range(TT, UNITS):
+            project(u, 0)
+        sum_squares(0)
+        sum_squares(1)
+        sum_squares(2)
         clamp(0, 2)
         sum_squares(3)
-        rg_v("c1", 256, 512)
-        project(4, 0)
         inverse_norm(0, 2)
-        rg_v("w0", 0, 256)
         clamp(2, 4)
-        project(5, 0)
-        scale("S", 0)
-        store_o(0)
-        project(6, 0)
-        project(7, 0)
-        quantise("c1", 0, 512)
+        scale_store_transpose(0)
         inverse_norm(2, 4)
-        scale("S", 1)
-        store_o(1)
-        transposes(0)
+        scale_store_transpose(1)
+        rg_v("c1", 256, 512)
+        rg_v("w0", 0, 256)
+        quantise("c1", 0, 512)
+        for u in range(TT, UNITS):
+            project(u, 1)
+        scale_store_transpose(2)
+        scale_store_transpose(3)
         rg_v("w0", 256, 512)
-        scale("S", 2)
-        store_o(2)
-        transposes(1)
+
         evacuate_transposed(vcopy, 0)
-        scale("S", 3)
-        store_o(3)
-        project(4, 1)
         quantise("w0", 0, 512)
-        project(5, 1)
-        project(6, 1)
-        sum_squares(4)
         evacuate_transposed(vcopy, 1)
-        project(7, 1)
-        transposes(2)
-        sum_squares(5)
         quantise_o(0)
-        transposes(3)
-        sum_squares(6)
-        evacuate_transposed(vcopy, 2)
         bilinear(0)
+        evacuate_transposed(vcopy, 2)
         quantise_o(1)
+        bilinear(1)
+        evacuate_transposed(vcopy, 3)
+        quantise_o(2)
+        bilinear(2)
+        sum_squares(4)
+        sum_squares(5)
+        sum_squares(6)
         clamp(4, 6)
         sum_squares(7)
-        evacuate_transposed(vcopy, 3)
-        bilinear(1)
         inverse_norm(4, 6)
-        quantise_o(2)
         clamp(6, 8)
-        scale("S", 4)
-        store_o(4)
-        copy_q(vcopy, 0)
-        store_q(0)
-        bilinear(2)
+        scale_store_transpose(4)
+        store_q(vcopy, 0)
         quantise_o(3)
-        inverse_norm(6, 8)
-        scale("S", 5)
-        store_o(5)
-        transposes(4)
-        copy_q(vcopy, 1)
-        store_q(1)
         bilinear(3)
+        inverse_norm(6, 8)
+        scale_store_transpose(5)
+        store_q(vcopy, 1)
+        scale_store_transpose(6)
+        scale_store_transpose(7)
         rg_v("w1", 0, 256)
-        scale("S", 6)
-        store_o(6)
-        transposes(5)
         rg_v("w1", 256, 512)
-        scale("S", 7)
-        store_o(7)
-        transposes(6)
-        copy_q(vcopy, 2)
-        store_q(2)
-        evacuate_transposed(scopy, 4)
-        transposes(7)
+        store_q(vcopy, 2)
         quantise("w1", 0, 512)
-        evacuate_transposed(scopy, 5)
+        evacuate_transposed(scopy, 4)
         quantise_o(4)
-        copy_q(vcopy, 3)
-        store_q(3)
-        evacuate_transposed(scopy, 6)
         bilinear(4)
+        store_q(vcopy, 3)
+        evacuate_transposed(scopy, 5)
         quantise_o(5)
-        evacuate_transposed(scopy, 7)
-        quantise_o(6)
-        copy_q(vcopy, 4)
-        store_q(4)
         bilinear(5)
+        evacuate_transposed(scopy, 6)
+        quantise_o(6)
         bilinear(6)
+        evacuate_transposed(scopy, 7)
         quantise_o(7)
-        copy_q(scopy, 5)
-        store_q(5)
-        copy_q(vcopy, 6)
-        store_q(6)
-        bilinear_half(7, 0, 7)
-        bilinear_half(7, 1, 3)
-        copy_store_half(vcopy, 7, 0)
-        copy_store_half(scopy, 7, 1)
+        bilinear(7)
+        store_q(vcopy, 4)
+        store_q(scopy, 5)
+        store_q(scopy, 6)
+        store_q(vcopy, 7)

@@ -185,9 +185,12 @@ def tile_mca_pa_kernel(tc, rgb, rgb_proj, atte_w, out_0, out_1):
             quantise("a1", i * P, (i + 1) * P)
             project(i, 1)
 
-        rg_v("c0", 0, 256)
-        rg_v("c0", 256, 512)
-        rg_v("c1", 0, 256)
+        rg_v("c0", 0, 128)
+        rg_v("c0", 128, 256)
+        rg_v("c0", 256, 384)
+        rg_v("c0", 384, 512)
+        rg_v("c1", 0, 128)
+        rg_v("c1", 128, 256)
         quantise("c0", 0, 512)
         for u in range(TT, UNITS):
             project(u, 0)
@@ -201,14 +204,17 @@ def tile_mca_pa_kernel(tc, rgb, rgb_proj, atte_w, out_0, out_1):
         scale_store_transpose(0)
         inverse_norm(2, 4)
         scale_store_transpose(1)
-        rg_v("c1", 256, 512)
-        rg_v("w0", 0, 256)
+        rg_v("c1", 256, 384)
+        rg_v("c1", 384, 512)
+        rg_v("w0", 0, 128)
+        rg_v("w0", 128, 256)
         quantise("c1", 0, 512)
         for u in range(TT, UNITS):
             project(u, 1)
         scale_store_transpose(2)
         scale_store_transpose(3)
-        rg_v("w0", 256, 512)
+        rg_v("w0", 256, 384)
+        rg_v("w0", 384, 512)
 
         evacuate_transposed(vcopy, 0)
         quantise("w0", 0, 512)
@@ -237,8 +243,10 @@ def tile_mca_pa_kernel(tc, rgb, rgb_proj, atte_w, out_0, out_1):
         store_q(vcopy, 1)
         scale_store_transpose(6)
         scale_store_transpose(7)
-        rg_v("w1", 0, 256)
-        rg_v("w1", 256, 512)
+        rg_v("w1", 0, 128)
+        rg_v("w1", 128, 256)
+        rg_v("w1", 256, 384)
+        rg_v("w1", 384, 512)
         store_q(vcopy, 2)
         quantise("w1", 0, 512)
         evacuate_transposed(scopy, 4)

from contextlib import ExitStack

import concourse.masks as masks
import concourse.mybir as mybir

F32 = mybir.dt.float32
BF16 = mybir.dt.bfloat16
U32 = mybir.dt.uint32
U8 = mybir.dt.uint8
FP8X4 = mybir.dt.float8_e4m3fn_x4
ACT = mybir.ActivationFunctionType

P = 128
PACK = 4
K_PASS = P * PACK
D, T, H, DH = 1024, 512, 2, 512
TT = T // P
UNITS = H * TT
FLOOR = 1e-24
FLOPS = 2 * H * T * D * DH + 2 * H * T * DH * DH


def tile_mca_pa_kernel(tc, rgb, rgb_proj, atte_w, out_0, out_1):
    nc = tc.nc
    with ExitStack() as ctx:
        keep = ctx.enter_context(tc.tile_pool(name="keep", bufs=1))
        junkp = ctx.enter_context(tc.tile_pool(name="junkp", bufs=2))
        psum = ctx.enter_context(tc.psum_pool(name="psum", bufs=1))

        rgb_rows = rgb.rearrange("n d t -> (n d) t")
        proj_rows = rgb_proj.rearrange("h d f -> (h d) f")
        w_view = atte_w.rearrange("h (j p) n -> h p j n", p=P)
        o_view = out_0.rearrange("n h (i p) f -> (n h i) p f", p=P)
        q_view = out_1.rearrange("n h (i p) f -> (n h i) p f", p=P)

        def k_first(rows, c):
            return rows[c * K_PASS : (c + 1) * K_PASS, :].rearrange("(p j) w -> p j w", j=PACK)

        sources = {
            "b0": k_first(proj_rows, 0),
            "a0": k_first(rgb_rows, 0),
            "b1": k_first(proj_rows, 1),
            "a1": k_first(rgb_rows, 1),
            "c0": k_first(proj_rows, 2),
            "c1": k_first(proj_rows, 3),
            "w0": w_view[0],
            "w1": w_view[1],
        }
        order = ["b0", "a0", "b1", "a1", "c0", "c1", "w0", "w1"]

        warm = keep.tile([P, 1], F32, name="warm")
        nc.vector.memset(warm[:], 1.0)
        nc.scalar.activation(out=warm[:], in_=warm[:], func=ACT.Abs_reciprocal_sqrt)

        raw, grouped, codes, scales = {}, {}, {}, {}
        for k in order:
            raw[k] = keep.tile([P, PACK, 512], BF16, name="raw_" + k)
            grouped[k] = keep.tile([P, 512, PACK], BF16, name="grp_" + k, align_bytes=64)
            codes[k] = keep.tile([P, 512], U32, name="cod_" + k, align_bytes=64)
            scales[k] = keep.tile([P, 512], U8, name="scl_" + k, align_bytes=64)
            nc.sync.dma_start(out=raw[k][:], in_=sources[k])

        ident = keep.tile([P, P], F32, name="ident")
        masks.make_identity(nc, ident[:])

        def regroup(engine_copy, k, lo, hi):
            engine_copy(
                out=grouped[k][:, lo:hi, :].rearrange("p (c i) j -> p c j i", i=4),
                in_=raw[k][:, :, lo:hi].rearrange("p j (c i) -> p c j i", i=4),
            )

        def rg_v(k, lo, hi):
            regroup(nc.vector.tensor_copy, k, lo, hi)

        def rg_s(k, lo, hi):
            regroup(nc.scalar.copy, k, lo, hi)

        def quantise(k, lo, hi):
            nc.vector.quantize_mx(
                out=codes[k][:, lo:hi].bitcast(FP8X4),
                scales=scales[k][:, lo:hi],
                in_=grouped[k][:, lo:hi, :].rearrange("p w j -> p (w j)"),
            )

        ssq = keep.tile([P, UNITS], F32, name="ssq")
        clamped = keep.tile([P, UNITS], F32, name="clamped")
        rnorm = keep.tile([P, UNITS], F32, name="rnorm")
        p_ps, x_ps, q_ps, o_sb, q_sb, og, oc, osc = {}, {}, {}, {}, {}, {}, {}, {}

        def project(u, c):
            h, i = divmod(u, TT)
            a, b = ("a%d" % c), (("b%d" if h == 0 else "c%d") % c)
            if c == 0:
                p_ps[u] = psum.tile([P, DH], F32, name="p%d" % u, tag="bank%d" % u)
            nc.tensor.matmul_mx(
                out=p_ps[u][:],
                lhsT=codes[a][:, i * P : (i + 1) * P].bitcast(FP8X4),
                lhsT_scale=scales[a][:, i * P : (i + 1) * P],
                rhs=codes[b][:].bitcast(FP8X4),
                rhs_scale=scales[b][:],
                start=(c == 0),
                stop=(c == 1),
            )

        def sum_squares(u):
            junk = junkp.tile([P, DH], BF16, name="junk")
            nc.scalar.activation(
                out=junk[:], in_=p_ps[u][:], func=ACT.Square, accum_out=ssq[:, u : u + 1]
            )

        def clamp(lo, hi):
            nc.scalar.activation(
                out=clamped[:, lo:hi], in_=ssq[:, lo:hi], func=ACT.Relu, bias=-FLOOR
            )

        def inverse_norm(lo, hi):
            nc.scalar.activation(
                out=rnorm[:, lo:hi], in_=clamped[:, lo:hi], func=ACT.Abs_reciprocal_sqrt, bias=FLOOR
            )

        def scale_store_transpose(u):
            o_sb[u] = keep.tile([P, DH], F32, name="o_sb%d" % u)
            nc.scalar.activation(
                out=o_sb[u][:], in_=p_ps[u][:], func=ACT.Copy, scale=rnorm[:, u : u + 1]
            )
            nc.sync.dma_start(out=o_view[u], in_=o_sb[u][:])
            x_ps[u] = psum.tile([P, PACK, P], F32, name="x%d" % u, tag="bank%d" % u)
            for j in range(PACK):
                nc.tensor.transpose(x_ps[u][:, j, :], o_sb[u][:, j * P : (j + 1) * P], ident[:])

        def evacuate_transposed(engine_copy, u):
            og[u] = keep.tile([P, P, PACK], BF16, name="og%d" % u, align_bytes=64)
            engine_copy(out=og[u][:], in_=x_ps[u][:].rearrange("p j t -> p t j"))

        def quantise_o(u):
            oc[u] = keep.tile([P, P], U32, name="oc%d" % u, align_bytes=64)
            osc[u] = keep.tile([P, P], U8, name="osc%d" % u, align_bytes=64)
            nc.vector.quantize_mx(
                out=oc[u][:].bitcast(FP8X4),
                scales=osc[u][:],
                in_=og[u][:].rearrange("p t j -> p (t j)"),
            )

        def bilinear(u):
            w = "w%d" % (u // TT)
            q_ps[u] = psum.tile([P, DH], F32, name="q%d" % u, tag="bank%d" % u)
            nc.tensor.matmul_mx(
                out=q_ps[u][:],
                lhsT=oc[u][:].bitcast(FP8X4),
                lhsT_scale=osc[u][:],
                rhs=codes[w][:].bitcast(FP8X4),
                rhs_scale=scales[w][:],
                start=True,
                stop=True,
            )

        def store_q(engine_copy, u):
            q_sb[u] = keep.tile([P, DH], F32, name="q_sb%d" % u)
            engine_copy(out=q_sb[u][:], in_=q_ps[u][:])
            nc.sync.dma_start(out=q_view[u], in_=q_sb[u][:])

        vcopy, scopy = nc.vector.tensor_copy, nc.scalar.copy

        rg_v("b0", 0, 256)
        rg_s("b0", 256, 512)
        quantise("b0", 0, 256)
        rg_v("a0", 0, 256)
        rg_s("a0", 256, 512)
        quantise("b0", 256, 512)
        quantise("a0", 0, 256)
        rg_v("b1", 0, 256)
        rg_s("b1", 256, 512)
        quantise("a0", 256, 512)
        for u in range(TT):
            project(u, 0)
        quantise("b1", 0, 256)
        rg_v("a1", 0, 128)
        rg_s("a1", 128, 256)
        quantise("b1", 256, 512)
        quantise("a1", 0, 128)
        project(0, 1)
        rg_v("a1", 256, 384)
        rg_s("a1", 384, 512)
        for i in range(1, TT):
            quantise("a1", i * P, (i + 1) * P)
            project(i, 1)

        rg_v("c0", 0, 128)
        rg_v("c0", 128, 256)
        rg_v("c0", 256, 384)
        rg_v("c0", 384, 512)
        rg_v("c1", 0, 128)
        rg_v("c1", 128, 256)
        quantise("c0", 0, 512)
        for u in range(TT, UNITS):
            project(u, 0)
        sum_squares(0)
        sum_squares(1)
        sum_squares(2)
        clamp(0, 2)
        sum_squares(3)
        inverse_norm(0, 2)
        clamp(2, 4)
        scale_store_transpose(0)
        inverse_norm(2, 4)
        scale_store_transpose(1)
        rg_v("c1", 256, 384)
        rg_v("c1", 384, 512)
        rg_v("w0", 0, 128)
        rg_v("w0", 128, 256)
        quantise("c1", 0, 512)
        for u in range(TT, UNITS):
            project(u, 1)
        scale_store_transpose(2)
        scale_store_transpose(3)
        rg_v("w0", 256, 384)
        rg_v("w0", 384, 512)

        evacuate_transposed(vcopy, 0)
        quantise("w0", 0, 512)
        evacuate_transposed(vcopy, 1)
        quantise_o(0)
        bilinear(0)
        evacuate_transposed(vcopy, 2)
        quantise_o(1)
        bilinear(1)
        evacuate_transposed(vcopy, 3)
        quantise_o(2)
        bilinear(2)
        sum_squares(4)
        sum_squares(5)
        sum_squares(6)
        clamp(4, 6)
        sum_squares(7)
        inverse_norm(4, 6)
        clamp(6, 8)
        scale_store_transpose(4)
        store_q(vcopy, 0)
        quantise_o(3)
        bilinear(3)
        inverse_norm(6, 8)
        scale_store_transpose(5)
        store_q(vcopy, 1)
        scale_store_transpose(6)
        scale_store_transpose(7)
        rg_v("w1", 0, 128)
        rg_v("w1", 128, 256)
        rg_v("w1", 256, 384)
        rg_v("w1", 384, 512)
        store_q(vcopy, 2)
        quantise("w1", 0, 512)
        evacuate_transposed(scopy, 4)
        quantise_o(4)
        bilinear(4)
        store_q(vcopy, 3)
        evacuate_transposed(scopy, 5)
        quantise_o(5)
        bilinear(5)
        evacuate_transposed(scopy, 6)
        quantise_o(6)
        bilinear(6)
        evacuate_transposed(scopy, 7)
        quantise_o(7)
        bilinear(7)
        store_q(vcopy, 4)
        store_q(scopy, 5)
        store_q(scopy, 6)
        store_q(vcopy, 7)
